import numpy as np
import ml_dtypes


def mxq(x, axis, fmt="e4m3"):
    dtype, down = {"e4m3": (ml_dtypes.float8_e4m3fn, 7), "e5m2": (ml_dtypes.float8_e5m2, 14)}[fmt]
    v = np.moveaxis(np.asarray(x, np.float32).astype(ml_dtypes.bfloat16).astype(np.float64), axis, -1)
    blocks = v.reshape(v.shape[:-1] + (-1, 32))
    amax = np.abs(blocks).max(-1, keepdims=True)
    byte = np.maximum(np.where(amax > 0, np.frexp(amax)[1] - 1 + 127, 0) - down, 1)
    scale = np.exp2(byte - 127.0)
    codes = (blocks / scale).astype(np.float32).astype(dtype).astype(np.float64)
    return np.moveaxis((codes * scale).reshape(v.shape), -1, axis)


WIDE = False


def mx_kscale(k):
    if not WIDE:
        return np.ones(k)
    levels = np.array([10, -10, 5, -5, 0])
    a = np.random.permutation(np.resize(levels, k // 512 * 4)).reshape(k // 512, 4)
    idx = np.arange(k)
    return np.exp2(a[idx // 512, idx % 128 // 32])


BF16 = ml_dtypes.bfloat16


def bf(x):
    return np.asarray(x, np.float32).astype(BF16)


def f64(x):
    return np.asarray(x).astype(np.float64)


B, H, W, NB, BS, F = 1, 16, 32, 8, 512, 512
C = NB * BS
SPARSITY = 0.01


def blockmm(a, w):
    r = np.moveaxis(a, 3, 0).reshape(NB, B * H * W, -1) @ w
    return np.moveaxis(r, 0, 1).reshape(B, H, W, NB, -1)


def setup_inputs():
    s = mx_kscale(F)
    return {"o1k": bf(np.maximum(np.random.standard_normal((B, H, W, NB, F)), 0.0) * 0.27 * s),
            "o1n": bf(np.maximum(np.random.standard_normal((B, H, W, NB, F)), 0.0) * 0.27 * s),
            "w2": bf(np.random.standard_normal((2, NB, F, BS)) * 0.7 / np.sqrt(F) / s[:, None] * s),
            "b2": bf(np.random.standard_normal((2, NB, BS)) * 0.05 * s)}


def reference(o1k, o1n, w2, b2):
    w2, b2 = f64(w2), f64(b2)
    o1kq = mxq(f64(o1k), 4, "e4m3")
    o1nq = mxq(f64(o1n), 4, "e4m3")
    w2a = mxq(w2[0] + w2[1], 1, "e4m3")
    w2b = mxq(w2[0] - w2[1], 1, "e4m3")
    o2k = 0.5 * (blockmm(o1kq, w2a) + blockmm(o1nq, w2b)) + b2[0]
    o2n = 0.5 * (blockmm(o1nq, w2a) + blockmm(mxq(o2k, 4, "e4m3"), w2b)) + b2[1]
    y = (o2k + o2n).reshape(B, H, W, C)
    return np.sign(y) * np.maximum(np.abs(y) - SPARSITY, 0.0)

@@ -1,0 +1,229 @@
+from contextlib import ExitStack
+
+import concourse.mybir as mybir
+from concourse.masks import make_identity
+
+F32 = mybir.dt.float32
+BF16 = mybir.dt.bfloat16
+I32 = mybir.dt.int32
+U32 = mybir.dt.uint32
+U8 = mybir.dt.uint8
+FP8X4 = mybir.dt.float8_e4m3fn_x4
+ALU = mybir.AluOpType
+ACT = mybir.ActivationFunctionType
+
+P = 128
+NB = 8
+T = 512
+F = 512
+TC = T // P
+LAM = 0.01
+FLOPS = 4 * NB * 2 * T * F * F
+ON_VECTOR = (("wb_g", 0), ("wb_g", 2), ("wb_g", 5))
+
+
+def tile_afno2d_pb_kernel(tc, o1k, o1n, w2, b2, out):
+    nc = tc.nc
+    xk_d = o1k.rearrange("b h w n f -> (b h w) n f")
+    xn_d = o1n.rearrange("b h w n f -> (b h w) n f")
+    out_d = out.rearrange("b h w (n o) -> (b h w) n o", n=NB)
+
+    with ExitStack() as ctx:
+        consts = ctx.enter_context(tc.tile_pool(name="consts", bufs=1))
+        loads = ctx.enter_context(tc.tile_pool(name="loads", bufs=3))
+        work = ctx.enter_context(tc.tile_pool(name="work", bufs=2))
+        codes = ctx.enter_context(tc.tile_pool(name="codes", bufs=3))
+        ypool = ctx.enter_context(tc.tile_pool(name="ypool", bufs=2))
+        ps_t = ctx.enter_context(tc.psum_pool(name="ps_t", bufs=2))
+        ps_s = ctx.enter_context(tc.psum_pool(name="ps_s", bufs=2))
+        ps_y = ctx.enter_context(tc.psum_pool(name="ps_y", bufs=4))
+
+        raw = {}
+        quant = {}
+
+        def load(nb):
+            xk = loads.tile([P, TC * F], BF16, name="xk")
+            xn = loads.tile([P, TC * F], BF16, name="xn")
+            w0 = loads.tile([P, 4 * F], BF16, name="w0")
+            w1 = loads.tile([P, 4 * F], BF16, name="w1")
+            nc.sync.dma_start(
+                out=w0[:].rearrange("p (u r) -> p u r", u=2),
+                in_=w2[0, nb, :, :].rearrange("(u p e) o -> p u (e o)", u=2, e=2),
+            )
+            nc.sync.dma_start(
+                out=w1[:].rearrange("p (u r) -> p u r", u=2),
+                in_=w2[1, nb, :, :].rearrange("(u p e) o -> p u (e o)", u=2, e=2),
+            )
+            nc.sync.dma_start(
+                out=xk[:].rearrange("p (c f) -> p c f", c=TC),
+                in_=xk_d[:, nb, :].rearrange("(c p) f -> p c f", p=P),
+            )
+            nc.sync.dma_start(
+                out=xn[:].rearrange("p (c f) -> p c f", c=TC),
+                in_=xn_d[:, nb, :].rearrange("(c p) f -> p c f", p=P),
+            )
+            raw[nb] = (xk, xn, w0, w1)
+
+        ident = consts.tile([P, P], F32, name="ident")
+        make_identity(nc, ident[:])
+        ones = consts.tile([P, P], BF16, name="ones")
+        nc.vector.memset(ones[:], 1.0)
+        brow = consts.tile([P, NB * F], BF16, name="brow")
+        nc.vector.memset(brow[:].bitcast(I32), 0)
+        nc.sync.dma_start(out=brow[0:2, :], in_=b2.rearrange("i n o -> i (n o)"))
+        btile = consts.tile([P, 2 * P], BF16, name="btile")
+        nc.vector.memset(btile[:].bitcast(I32), 0)
+        nc.sync.dma_start(
+            out=btile[0 : 2 * NB, :],
+            in_=b2[0, :, :].rearrange("n (u r) -> (n u) r", u=2),
+        )
+        load(0)
+        load(1)
+        pbt = ps_t.tile([P, 4 * P], F32, name="pt")
+        nc.tensor.transpose(out=pbt[:, 0:P], in_=btile[:].bitcast(F32), identity=ident[:])
+        bsb = consts.tile([P, 2 * NB], F32, name="bsb")
+        nc.vector.tensor_copy(out=bsb[:], in_=pbt[:, 0 : 2 * NB])
+        bias0 = consts.tile([P, 4 * NB], F32, name="bias0")
+        nc.vector.tensor_copy(out=bias0[:], in_=bsb[:].bitcast(BF16))
+        bias_y = consts.tile([P, NB * F], F32, name="bias_y")
+        for n in range(NB):
+            pb = ps_s.tile([P, F], F32, name="ps1")
+            nc.tensor.matmul(
+                out=pb[:], lhsT=ones[:], rhs=brow[:, n * F : (n + 1) * F], start=True, stop=True
+            )
+            nc.scalar.activation(
+                out=bias_y[:, n * F : (n + 1) * F], in_=pb[:], func=ACT.Identity, bias=-LAM, scale=1.0
+            )
+
+        def quantise(src, tag):
+            c = codes.tile([P, F], U32, name=tag + "c", align_bytes=64)
+            s = codes.tile([P, F], U8, name=tag + "s", align_bytes=64)
+            nc.vector.quantize_mx(out=c[:].bitcast(FP8X4), scales=s[:], in_=src[:])
+            return (c, s)
+
+        def stage_a(nb):
+            xk, xn, w0, w1 = raw[nb]
+            wa_r = work.tile([P, 4 * F], BF16, name="wa_r")
+            wb_r = work.tile([P, 4 * F], BF16, name="wb_r")
+            nc.vector.tensor_tensor(out=wa_r[:], in0=w0[:], in1=w1[:], op=ALU.add)
+            nc.vector.tensor_tensor(out=wb_r[:], in0=w0[:], in1=w1[:], op=ALU.subtract)
+            grouped = []
+            for x, tag in ((xk, "xkg"), (xn, "xng")):
+                xw = x[:].bitcast(F32)
+                g = work.tile([P, 4 * T], BF16, name=tag, align_bytes=64)
+                gw = g[:].bitcast(F32)
+                for h in range(2):
+                    pt = ps_t.tile([P, 4 * P], F32, name="pt")
+                    for cl in range(2):
+                        for u in range(2):
+                            c = 2 * h + cl
+                            nc.tensor.transpose(
+                                out=pt[:, (2 * cl + u) * P : (2 * cl + u + 1) * P],
+                                in_=xw[:, c * 256 + u * P : c * 256 + (u + 1) * P],
+                                identity=ident[:],
+                            )
+                    nc.scalar.copy(
+                        out=gw[:, h * 512 : (h + 1) * 512].rearrange("p (c t u) -> p c t u", c=2, u=2),
+                        in_=pt[:].rearrange("p (c u t) -> p c t u", c=2, u=2),
+                    )
+                grouped.append(g)
+            wg = []
+            for r, tag in ((wa_r, "wa_g"), (wb_r, "wb_g")):
+                g = work.tile([P, 4 * F], BF16, name=tag, align_bytes=64)
+                if (tag, nb) in ON_VECTOR:
+                    nc.vector.tensor_copy(
+                        out=g[:].rearrange("p (e q t) -> p e q t", e=2, t=4),
+                        in_=r[:].rearrange("p (t q e) -> p e q t", e=2, t=4),
+                    )
+                else:
+                    nc.scalar.copy(
+                        out=g[:].rearrange("p (e q t) -> p e q t", e=2, t=4),
+                        in_=r[:].rearrange("p (t q e) -> p e q t", e=2, t=4),
+                    )
+                wg.append(g)
+            quant[nb] = (
+                quantise(grouped[0], "xk"),
+                quantise(grouped[1], "xn"),
+                quantise(wg[0], "wa"),
+                quantise(wg[1], "wb"),
+            )
+
+        def mx(acc, a, acols, b, start, stop):
+            nc.tensor.matmul_mx(
+                out=acc[:],
+                lhsT=a[0][:, acols].bitcast(FP8X4),
+                lhsT_scale=a[1][:, acols],
+                rhs=b[0][:].bitcast(FP8X4),
+                rhs_scale=b[1][:],
+                start=start,
+                stop=stop,
+            )
+
+        def stage_b(nb):
+            qxk, qxn, qwa, qwb = quant[nb]
+            o2b = work.tile([P, 4 * T], BF16, name="o2b")
+            for c in range(4):
+                t4 = 2 * (c % 2) + c // 2
+                cols = slice(c * P, (c + 1) * P)
+                ps1 = ps_s.tile([P, T], F32, name="ps1")
+                mx(ps1, qwa, cols, qxk, True, False)
+                mx(ps1, qwb, cols, qxn, False, True)
+                nc.scalar.activation(
+                    out=o2b[:, t4 * T : (t4 + 1) * T],
+                    in_=ps1[:],
+                    func=ACT.Identity,
+                    bias=bias0[:, nb * 4 + t4 : nb * 4 + t4 + 1],
+                    scale=0.5,
+                )
+            o2g = work.tile([P, 4 * T], BF16, name="o2g", align_bytes=64)
+            nc.vector.tensor_copy(
+                out=o2g[:].rearrange("p (t j) -> p t j", j=4),
+                in_=o2b[:].rearrange("p (j t) -> p t j", j=4),
+            )
+            return quantise(o2g, "o2")
+
+        def stage_c(nb, qo2):
+            qxk, qxn, qwa, qwb = quant[nb]
+            pys = []
+            for c in range(TC):
+                cols = slice(c * P, (c + 1) * P)
+                py = ps_y.tile([P, F], F32, name="py")
+                mx(py, qxk, cols, qwa, True, False)
+                mx(py, qxn, cols, qwb, False, False)
+                mx(py, qxn, cols, qwa, False, False)
+                pys.append(py)
+            for c in range(TC):
+                cols = slice(c * P, (c + 1) * P)
+                mx(pys[c], qo2, cols, qwb, False, True)
+            za = ypool.tile([P, TC * F], F32, name="za")
+            r2 = ypool.tile([P, TC * F], F32, name="r2")
+            for c in range(TC):
+                nc.vector.scalar_tensor_tensor(
+                    out=za[:, c * F : (c + 1) * F].rearrange("p (q e) -> p q e", e=2),
+                    in0=pys[c][:].rearrange("p (e q) -> p q e", e=2),
+                    scalar=0.5,
+                    in1=bias_y[:, nb * F : (nb + 1) * F].rearrange("p (q e) -> p q e", e=2),
+                    op0=ALU.mult,
+                    op1=ALU.add,
+                )
+            for h in range(2):
+                sl = slice(h * 2 * F, (h + 1) * 2 * F)
+                nc.scalar.activation(
+                    out=r2[:, sl], in_=za[:, sl], func=ACT.Relu, bias=-2.0 * LAM, scale=-1.0
+                )
+                nc.vector.scalar_tensor_tensor(
+                    out=r2[:, sl], in0=za[:, sl], scalar=0.0, in1=r2[:, sl], op0=ALU.max, op1=ALU.subtract
+                )
+                nc.gpsimd.dma_start(
+                    out=out_d[h * 2 * P : (h + 1) * 2 * P, nb, :].rearrange("(c p) o -> p c o", p=P),
+                    in_=r2[:, sl].rearrange("p (c o) -> p c o", c=2),
+                )
+
+        stage_a(0)
+        for nb in range(NB):
+            if nb + 2 < NB:
+                load(nb + 2)
+            if nb + 1 < NB:
+                stage_a(nb + 1)
+            qo2 = stage_b(nb)
+            stage_c(nb, qo2)

@@ -19,16 +19,19 @@ F = 512
 TC = T // P
 LAM = 0.01
 FLOPS = 4 * NB * 2 * T * F * F
-ON_VECTOR = (("wb_g", 0), ("wb_g", 2), ("wb_g", 5))
+VECTOR_REGROUPS = (0,)
 
 
 def tile_afno2d_pb_kernel(tc, o1k, o1n, w2, b2, out):
     nc = tc.nc
-    xk_d = o1k.rearrange("b h w n f -> (b h w) n f")
-    xn_d = o1n.rearrange("b h w n f -> (b h w) n f")
+    x_d = (
+        o1k.rearrange("b h w n f -> (b h w) n f"),
+        o1n.rearrange("b h w n f -> (b h w) n f"),
+    )
     out_d = out.rearrange("b h w (n o) -> (b h w) n o", n=NB)
 
     with ExitStack() as ctx:
+        ctx.enter_context(tc.manual_schedule())
         consts = ctx.enter_context(tc.tile_pool(name="consts", bufs=1))
         loads = ctx.enter_context(tc.tile_pool(name="loads", bufs=3))
         work = ctx.enter_context(tc.tile_pool(name="work", bufs=2))
@@ -38,31 +41,10 @@ def tile_afno2d_pb_kernel(tc, o1k, o1n, w2, b2, out):
         ps_s = ctx.enter_context(tc.psum_pool(name="ps_s", bufs=2))
         ps_y = ctx.enter_context(tc.psum_pool(name="ps_y", bufs=4))
 
-        raw = {}
-        quant = {}
+        st = {}
 
-        def load(nb):
-            xk = loads.tile([P, TC * F], BF16, name="xk")
-            xn = loads.tile([P, TC * F], BF16, name="xn")
-            w0 = loads.tile([P, 4 * F], BF16, name="w0")
-            w1 = loads.tile([P, 4 * F], BF16, name="w1")
-            nc.sync.dma_start(
-                out=w0[:].rearrange("p (u r) -> p u r", u=2),
-                in_=w2[0, nb, :, :].rearrange("(u p e) o -> p u (e o)", u=2, e=2),
-            )
-            nc.sync.dma_start(
-                out=w1[:].rearrange("p (u r) -> p u r", u=2),
-                in_=w2[1, nb, :, :].rearrange("(u p e) o -> p u (e o)", u=2, e=2),
-            )
-            nc.sync.dma_start(
-                out=xk[:].rearrange("p (c f) -> p c f", c=TC),
-                in_=xk_d[:, nb, :].rearrange("(c p) f -> p c f", p=P),
-            )
-            nc.sync.dma_start(
-                out=xn[:].rearrange("p (c f) -> p c f", c=TC),
-                in_=xn_d[:, nb, :].rearrange("(c p) f -> p c f", p=P),
-            )
-            raw[nb] = (xk, xn, w0, w1)
+        def ok(b):
+            return 0 <= b < NB
 
         ident = consts.tile([P, P], F32, name="ident")
         make_identity(nc, ident[:])
@@ -77,8 +59,29 @@ def tile_afno2d_pb_kernel(tc, o1k, o1n, w2, b2, out):
             out=btile[0 : 2 * NB, :],
             in_=b2[0, :, :].rearrange("n (u r) -> (n u) r", u=2),
         )
-        load(0)
-        load(1)
+
+        def load_w(b):
+            if not ok(b):
+                return
+            for i in range(2):
+                w = loads.tile([P, 4 * F], BF16, name="w%d" % i)
+                nc.sync.dma_start(
+                    out=w[:].rearrange("p (u r) -> p u r", u=2),
+                    in_=w2[i, b, :, :].rearrange("(u p e) o -> p u (e o)", u=2, e=2),
+                )
+                st["w", i, b] = w
+
+        def load_x(b):
+            if not ok(b):
+                return
+            for i in range(2):
+                x = loads.tile([P, TC * F], BF16, name="x%d" % i)
+                nc.sync.dma_start(
+                    out=x[:].rearrange("p (c f) -> p c f", c=TC),
+                    in_=x_d[i][:, b, :].rearrange("(c p) f -> p c f", p=P),
+                )
+                st["x", i, b] = x
+
         pbt = ps_t.tile([P, 4 * P], F32, name="pt")
         nc.tensor.transpose(out=pbt[:, 0:P], in_=btile[:].bitcast(F32), identity=ident[:])
         bsb = consts.tile([P, 2 * NB], F32, name="bsb")
@@ -87,143 +90,216 @@ def tile_afno2d_pb_kernel(tc, o1k, o1n, w2, b2, out):
         nc.vector.tensor_copy(out=bias0[:], in_=bsb[:].bitcast(BF16))
         bias_y = consts.tile([P, NB * F], F32, name="bias_y")
         for n in range(NB):
-            pb = ps_s.tile([P, F], F32, name="ps1")
+            pb = ps_y.tile([P, F], F32, name="py")
             nc.tensor.matmul(
                 out=pb[:], lhsT=ones[:], rhs=brow[:, n * F : (n + 1) * F], start=True, stop=True
             )
-            nc.scalar.activation(
-                out=bias_y[:, n * F : (n + 1) * F], in_=pb[:], func=ACT.Identity, bias=-LAM, scale=1.0
-            )
+            if n % 2 == 0:
+                nc.scalar.activation(
+                    out=bias_y[:, n * F : (n + 1) * F], in_=pb[:], func=ACT.Identity, bias=-LAM, scale=1.0
+                )
+            else:
+                nc.vector.tensor_scalar_add(out=bias_y[:, n * F : (n + 1) * F], in0=pb[:], scalar1=-LAM)
 
-        def quantise(src, tag):
-            c = codes.tile([P, F], U32, name=tag + "c", align_bytes=64)
-            s = codes.tile([P, F], U8, name=tag + "s", align_bytes=64)
+        def add_sub(b, which):
+            if not ok(b):
+                return
+            r = work.tile([P, 4 * F], BF16, name="wr%d" % which)
+            nc.vector.tensor_tensor(
+                out=r[:],
+                in0=st["w", 0, b][:],
+                in1=st["w", 1, b][:],
+                op=(ALU.add if which == 0 else ALU.subtract),
+            )
+            st["wr", which, b] = r
+
+        def regroup_w(b, which, e, engine):
+            if not ok(b) or (engine == "v") != (b in VECTOR_REGROUPS):
+                return
+            if which == 0 and e == 0:
+                st["wg", b] = work.tile([P, 8 * F], BF16, name="wg", align_bytes=64)
+            g = st["wg", b][:, which * 4 * F : (which + 1) * 4 * F]
+            dst = g.rearrange("p (e c i t) -> p e c t i", e=2, i=4, t=4)[:, e]
+            src = st["wr", which, b][:].rearrange("p (t c i e) -> p e c t i", t=4, i=4, e=2)[:, e]
+            if engine == "v":
+                nc.vector.tensor_copy(out=dst, in_=src)
+            else:
+                nc.scalar.copy(out=dst, in_=src)
+
+        def transposes(b, i):
+            if not ok(b):
+                return
+            xw = st["x", i, b][:].bitcast(F32)
+            for h in range(2):
+                pt = ps_t.tile([P, 4 * P], F32, name="pt")
+                for cl in range(2):
+                    for u in range(2):
+                        c = 2 * h + cl
+                        nc.tensor.transpose(
+                            out=pt[:, (2 * cl + u) * P : (2 * cl + u + 1) * P],
+                            in_=xw[:, c * 256 + u * P : c * 256 + (u + 1) * P],
+                            identity=ident[:],
+                        )
+                st["pt", i, h, b] = pt
+
+        def evac_x(b, i):
+            if not ok(b):
+                return
+            if i == 0:
+                st["xg", b] = work.tile([P, 8 * T], BF16, name="xg", align_bytes=64)
+            gw = st["xg", b][:].bitcast(F32)
+            for h in range(2):
+                lo = i * 1024 + h * 512
+                nc.scalar.copy(
+                    out=gw[:, lo : lo + 512].rearrange("p (c t u) -> p c t u", c=2, u=2),
+                    in_=st["pt", i, h, b][:].rearrange("p (c u t) -> p c t u", c=2, u=2),
+                )
+
+        def quantise(src, tag, width):
+            c = codes.tile([P, width], U32, name=tag + "c", align_bytes=64)
+            s = codes.tile([P, width], U8, name=tag + "s", align_bytes=64)
             nc.vector.quantize_mx(out=c[:].bitcast(FP8X4), scales=s[:], in_=src[:])
             return (c, s)
 
-        def stage_a(nb):
-            xk, xn, w0, w1 = raw[nb]
-            wa_r = work.tile([P, 4 * F], BF16, name="wa_r")
-            wb_r = work.tile([P, 4 * F], BF16, name="wb_r")
-            nc.vector.tensor_tensor(out=wa_r[:], in0=w0[:], in1=w1[:], op=ALU.add)
-            nc.vector.tensor_tensor(out=wb_r[:], in0=w0[:], in1=w1[:], op=ALU.subtract)
-            grouped = []
-            for x, tag in ((xk, "xkg"), (xn, "xng")):
-                xw = x[:].bitcast(F32)
-                g = work.tile([P, 4 * T], BF16, name=tag, align_bytes=64)
-                gw = g[:].bitcast(F32)
-                for h in range(2):
-                    pt = ps_t.tile([P, 4 * P], F32, name="pt")
-                    for cl in range(2):
-                        for u in range(2):
-                            c = 2 * h + cl
-                            nc.tensor.transpose(
-                                out=pt[:, (2 * cl + u) * P : (2 * cl + u + 1) * P],
-                                in_=xw[:, c * 256 + u * P : c * 256 + (u + 1) * P],
-                                identity=ident[:],
-                            )
-                    nc.scalar.copy(
-                        out=gw[:, h * 512 : (h + 1) * 512].rearrange("p (c t u) -> p c t u", c=2, u=2),
-                        in_=pt[:].rearrange("p (c u t) -> p c t u", c=2, u=2),
-                    )
-                grouped.append(g)
-            wg = []
-            for r, tag in ((wa_r, "wa_g"), (wb_r, "wb_g")):
-                g = work.tile([P, 4 * F], BF16, name=tag, align_bytes=64)
-                if (tag, nb) in ON_VECTOR:
-                    nc.vector.tensor_copy(
-                        out=g[:].rearrange("p (e q t) -> p e q t", e=2, t=4),
-                        in_=r[:].rearrange("p (t q e) -> p e q t", e=2, t=4),
-                    )
-                else:
-                    nc.scalar.copy(
-                        out=g[:].rearrange("p (e q t) -> p e q t", e=2, t=4),
-                        in_=r[:].rearrange("p (t q e) -> p e q t", e=2, t=4),
-                    )
-                wg.append(g)
-            quant[nb] = (
-                quantise(grouped[0], "xk"),
-                quantise(grouped[1], "xn"),
-                quantise(wg[0], "wa"),
-                quantise(wg[1], "wb"),
-            )
+        def quantise_xw(b):
+            if not ok(b):
+                return
+            st["qx", b] = quantise(st["xg", b], "x", 2 * T)
+            st["qw", b] = quantise(st["wg", b], "w", 2 * F)
 
-        def mx(acc, a, acols, b, start, stop):
+        def mx(acc, a, a_lo, b_, b_lo, start, stop):
             nc.tensor.matmul_mx(
                 out=acc[:],
-                lhsT=a[0][:, acols].bitcast(FP8X4),
-                lhsT_scale=a[1][:, acols],
-                rhs=b[0][:].bitcast(FP8X4),
-                rhs_scale=b[1][:],
+                lhsT=a[0][:, a_lo : a_lo + P].bitcast(FP8X4),
+                lhsT_scale=a[1][:, a_lo : a_lo + P],
+                rhs=b_[0][:, b_lo : b_lo + 512].bitcast(FP8X4),
+                rhs_scale=b_[1][:, b_lo : b_lo + 512],
                 start=start,
                 stop=stop,
             )
 
-        def stage_b(nb):
-            qxk, qxn, qwa, qwb = quant[nb]
-            o2b = work.tile([P, 4 * T], BF16, name="o2b")
-            for c in range(4):
-                t4 = 2 * (c % 2) + c // 2
-                cols = slice(c * P, (c + 1) * P)
+        def stage1(b, chunks):
+            if not ok(b):
+                return
+            qx, qw = st["qx", b], st["qw", b]
+            for c in chunks:
                 ps1 = ps_s.tile([P, T], F32, name="ps1")
-                mx(ps1, qwa, cols, qxk, True, False)
-                mx(ps1, qwb, cols, qxn, False, True)
+                mx(ps1, qw, c * P, qx, 0, True, False)
+                mx(ps1, qw, F + c * P, qx, T, False, True)
+                st["ps1", c, b] = ps1
+
+        def evac1(b, chunks):
+            if not ok(b):
+                return
+            if chunks[0] == 0:
+                st["o2b", b] = work.tile([P, 4 * T], BF16, name="o2b")
+            for c in chunks:
+                t4 = 2 * (c % 2) + c // 2
                 nc.scalar.activation(
-                    out=o2b[:, t4 * T : (t4 + 1) * T],
-                    in_=ps1[:],
+                    out=st["o2b", b][:, t4 * T : (t4 + 1) * T],
+                    in_=st["ps1", c, b][:],
                     func=ACT.Identity,
-                    bias=bias0[:, nb * 4 + t4 : nb * 4 + t4 + 1],
+                    bias=bias0[:, b * 4 + t4 : b * 4 + t4 + 1],
                     scale=0.5,
                 )
+
+        def regroup_o2(b):
+            if not ok(b):
+                return
             o2g = work.tile([P, 4 * T], BF16, name="o2g", align_bytes=64)
             nc.vector.tensor_copy(
-                out=o2g[:].rearrange("p (t j) -> p t j", j=4),
-                in_=o2b[:].rearrange("p (j t) -> p t j", j=4),
+                out=o2g[:].rearrange("p (c i j) -> p c j i", i=4, j=4),
+                in_=st["o2b", b][:].rearrange("p (j c i) -> p c j i", i=4, j=4),
             )
-            return quantise(o2g, "o2")
+            st["o2g", b] = o2g
 
-        def stage_c(nb, qo2):
-            qxk, qxn, qwa, qwb = quant[nb]
-            pys = []
+        def quantise_o2(b):
+            if not ok(b):
+                return
+            st["qo", b] = quantise(st["o2g", b], "o", T)
+
+        def y_first(b):
+            if not ok(b):
+                return
+            qx, qw = st["qx", b], st["qw", b]
             for c in range(TC):
-                cols = slice(c * P, (c + 1) * P)
                 py = ps_y.tile([P, F], F32, name="py")
-                mx(py, qxk, cols, qwa, True, False)
-                mx(py, qxn, cols, qwb, False, False)
-                mx(py, qxn, cols, qwa, False, False)
-                pys.append(py)
+                mx(py, qx, c * P, qw, 0, True, False)
+                mx(py, qx, T + c * P, qw, F, False, False)
+                mx(py, qx, T + c * P, qw, 0, False, False)
+                st["py", c, b] = py
+
+        def y_last(b):
+            if not ok(b):
+                return
             for c in range(TC):
-                cols = slice(c * P, (c + 1) * P)
-                mx(pys[c], qo2, cols, qwb, False, True)
+                mx(st["py", c, b], st["qo", b], c * P, st["qw", b], F, False, True)
+
+        def y_bias(b):
+            if not ok(b):
+                return
             za = ypool.tile([P, TC * F], F32, name="za")
-            r2 = ypool.tile([P, TC * F], F32, name="r2")
             for c in range(TC):
                 nc.vector.scalar_tensor_tensor(
                     out=za[:, c * F : (c + 1) * F].rearrange("p (q e) -> p q e", e=2),
-                    in0=pys[c][:].rearrange("p (e q) -> p q e", e=2),
+                    in0=st["py", c, b][:].rearrange("p (e q) -> p q e", e=2),
                     scalar=0.5,
-                    in1=bias_y[:, nb * F : (nb + 1) * F].rearrange("p (q e) -> p q e", e=2),
+                    in1=bias_y[:, b * F : (b + 1) * F].rearrange("p (q e) -> p q e", e=2),
                     op0=ALU.mult,
                     op1=ALU.add,
                 )
-            for h in range(2):
-                sl = slice(h * 2 * F, (h + 1) * 2 * F)
-                nc.scalar.activation(
-                    out=r2[:, sl], in_=za[:, sl], func=ACT.Relu, bias=-2.0 * LAM, scale=-1.0
-                )
-                nc.vector.scalar_tensor_tensor(
-                    out=r2[:, sl], in0=za[:, sl], scalar=0.0, in1=r2[:, sl], op0=ALU.max, op1=ALU.subtract
-                )
-                nc.gpsimd.dma_start(
-                    out=out_d[h * 2 * P : (h + 1) * 2 * P, nb, :].rearrange("(c p) o -> p c o", p=P),
-                    in_=r2[:, sl].rearrange("p (c o) -> p c o", c=2),
-                )
+            st["za", b] = za
 
-        stage_a(0)
-        for nb in range(NB):
-            if nb + 2 < NB:
-                load(nb + 2)
-            if nb + 1 < NB:
-                stage_a(nb + 1)
-            qo2 = stage_b(nb)
-            stage_c(nb, qo2)
+        def y_neg(b, h):
+            if not ok(b):
+                return
+            if h == 0:
+                st["r2", b] = ypool.tile([P, TC * F], F32, name="r2")
+            sl = slice(h * 2 * F, (h + 1) * 2 * F)
+            nc.scalar.activation(
+                out=st["r2", b][:, sl], in_=st["za", b][:, sl], func=ACT.Relu, bias=-2.0 * LAM, scale=-1.0
+            )
+
+        def y_out(b, h):
+            if not ok(b):
+                return
+            sl = slice(h * 2 * F, (h + 1) * 2 * F)
+            r2 = st["r2", b]
+            nc.vector.scalar_tensor_tensor(
+                out=r2[:, sl], in0=st["za", b][:, sl], scalar=0.0, in1=r2[:, sl], op0=ALU.max, op1=ALU.subtract
+            )
+            nc.sync.dma_start(
+                out=out_d[h * 2 * P : (h + 1) * 2 * P, b, :].rearrange("(c p) o -> p c o", p=P),
+                in_=r2[:, sl].rearrange("p (c o) -> p c o", c=2),
+            )
+
+        for i in range(-4, NB + 1):
+            load_x(i + 3)
+            load_w(i + 4)
+            transposes(i + 2, 0)
+            evac1(i, (0, 1))
+            stage1(i, (2, 3))
+            quantise_xw(i + 1)
+            y_neg(i - 1, 0)
+            evac1(i, (2, 3))
+            y_first(i)
+            add_sub(i + 3, 0)
+            y_neg(i - 1, 1)
+            y_out(i - 1, 0)
+            regroup_o2(i)
+            stage1(i + 1, (0, 1))
+            regroup_w(i + 2, 0, 0, "s")
+            evac_x(i + 2, 0)
+            y_out(i - 1, 1)
+            quantise_o2(i)
+            transposes(i + 2, 1)
+            regroup_w(i + 2, 0, 1, "s")
+            regroup_w(i + 2, 1, 0, "s")
+            evac_x(i + 2, 1)
+            regroup_w(i + 2, 1, 1, "s")
+            add_sub(i + 3, 1)
+            for which in range(2):
+                for e in range(2):
+                    regroup_w(i + 3, which, e, "v")
+            y_last(i)
+            y_bias(i)

@@ -280,26 +280,26 @@ def tile_afno2d_pb_kernel(tc, o1k, o1n, w2, b2, out):
             evac1(i, (0, 1))
             stage1(i, (2, 3))
             quantise_xw(i + 1)
+            regroup_w(i + 2, 0, 0, "s")
             y_neg(i - 1, 0)
+            y_out(i - 1, 0)
             evac1(i, (2, 3))
             y_first(i)
-            add_sub(i + 3, 0)
-            y_neg(i - 1, 1)
-            y_out(i - 1, 0)
             regroup_o2(i)
-            stage1(i + 1, (0, 1))
-            regroup_w(i + 2, 0, 0, "s")
             evac_x(i + 2, 0)
-            y_out(i - 1, 1)
-            quantise_o2(i)
             transposes(i + 2, 1)
+            stage1(i + 1, (0, 1))
+            add_sub(i + 3, 0)
+            quantise_o2(i)
+            y_neg(i - 1, 1)
+            y_out(i - 1, 1)
+            y_last(i)
             regroup_w(i + 2, 0, 1, "s")
             regroup_w(i + 2, 1, 0, "s")
-            evac_x(i + 2, 1)
             regroup_w(i + 2, 1, 1, "s")
             add_sub(i + 3, 1)
             for which in range(2):
                 for e in range(2):
                     regroup_w(i + 3, which, e, "v")
-            y_last(i)
+            evac_x(i + 2, 1)
             y_bias(i)

@@ -114,9 +114,10 @@ def tile_afno2d_pb_kernel(tc, o1k, o1n, w2, b2, out):
             st["wr", which, b] = r
 
         def regroup_w(b, which, e, engine):
-            if not ok(b) or (engine == "v") != (b in VECTOR_REGROUPS):
+            on_vector = b in VECTOR_REGROUPS or (which == 1 and e == 1)
+            if not ok(b) or (engine == "v") != on_vector:
                 return
-            if which == 0 and e == 0:
+            if ("wg", b) not in st:
                 st["wg", b] = work.tile([P, 8 * F], BF16, name="wg", align_bytes=64)
             g = st["wg", b][:, which * 4 * F : (which + 1) * 4 * F]
             dst = g.rearrange("p (e c i t) -> p e c t i", e=2, i=4, t=4)[:, e]
@@ -250,28 +251,36 @@ def tile_afno2d_pb_kernel(tc, o1k, o1n, w2, b2, out):
                 )
             st["za", b] = za
 
+        def y_pieces(b, h):
+            n = 2 if b == NB - 1 else 1
+            w = 2 // n
+            return [
+                (slice((2 * h + k * w) * F, (2 * h + (k + 1) * w) * F), slice((2 * h + k * w) * P, (2 * h + (k + 1) * w) * P))
+                for k in range(n)
+            ]
+
         def y_neg(b, h):
             if not ok(b):
                 return
             if h == 0:
                 st["r2", b] = ypool.tile([P, TC * F], F32, name="r2")
-            sl = slice(h * 2 * F, (h + 1) * 2 * F)
-            nc.scalar.activation(
-                out=st["r2", b][:, sl], in_=st["za", b][:, sl], func=ACT.Relu, bias=-2.0 * LAM, scale=-1.0
-            )
+            for sl, rows in y_pieces(b, h):
+                nc.scalar.activation(
+                    out=st["r2", b][:, sl], in_=st["za", b][:, sl], func=ACT.Relu, bias=-2.0 * LAM, scale=-1.0
+                )
 
         def y_out(b, h):
             if not ok(b):
                 return
-            sl = slice(h * 2 * F, (h + 1) * 2 * F)
             r2 = st["r2", b]
-            nc.vector.scalar_tensor_tensor(
-                out=r2[:, sl], in0=st["za", b][:, sl], scalar=0.0, in1=r2[:, sl], op0=ALU.max, op1=ALU.subtract
-            )
-            nc.sync.dma_start(
-                out=out_d[h * 2 * P : (h + 1) * 2 * P, b, :].rearrange("(c p) o -> p c o", p=P),
-                in_=r2[:, sl].rearrange("p (c o) -> p c o", c=2),
-            )
+            for sl, rows in y_pieces(b, h):
+                nc.vector.scalar_tensor_tensor(
+                    out=r2[:, sl], in0=st["za", b][:, sl], scalar=0.0, in1=r2[:, sl], op0=ALU.max, op1=ALU.subtract
+                )
+                nc.sync.dma_start(
+                    out=out_d[rows, b, :].rearrange("(c p) o -> p c o", p=P),
+                    in_=r2[:, sl].rearrange("p (c o) -> p c o", o=F),
+                )
 
         for i in range(-4, NB + 1):
             load_x(i + 3)

@@ -52,13 +52,34 @@ def tile_afno2d_pb_kernel(tc, o1k, o1n, w2, b2, out):
         nc.vector.memset(ones[:], 1.0)
         brow = consts.tile([P, NB * F], BF16, name="brow")
         nc.vector.memset(brow[:].bitcast(I32), 0)
-        nc.sync.dma_start(out=brow[0:2, :], in_=b2.rearrange("i n o -> i (n o)"))
         btile = consts.tile([P, 2 * P], BF16, name="btile")
         nc.vector.memset(btile[:].bitcast(I32), 0)
-        nc.sync.dma_start(
-            out=btile[0 : 2 * NB, :],
-            in_=b2[0, :, :].rearrange("n (u r) -> (n u) r", u=2),
-        )
+        bsb = consts.tile([P, 2 * NB], F32, name="bsb")
+        bias0 = consts.tile([P, 4 * NB], F32, name="bias0")
+        bias_y = consts.tile([P, NB * F], F32, name="bias_y")
+
+        def load_bias():
+            nc.sync.dma_start(out=brow[0:2, :], in_=b2.rearrange("i n o -> i (n o)"))
+            nc.sync.dma_start(
+                out=btile[0 : 2 * NB, :],
+                in_=b2[0, :, :].rearrange("n (u r) -> (n u) r", u=2),
+            )
+
+        def bias_columns():
+            pbt = ps_s.tile([P, T], F32, name="ps1")
+            nc.tensor.transpose(out=pbt[:, 0:P], in_=btile[:].bitcast(F32), identity=ident[:])
+            nc.vector.tensor_copy(out=bsb[:], in_=pbt[:, 0 : 2 * NB])
+            nc.vector.tensor_copy(out=bias0[:], in_=bsb[:].bitcast(BF16))
+
+        def bias_rows(blocks):
+            for n in blocks:
+                pb = ps_y.tile([P, F], F32, name="py")
+                nc.tensor.matmul(
+                    out=pb[:], lhsT=ones[:], rhs=brow[:, n * F : (n + 1) * F], start=True, stop=True
+                )
+                nc.scalar.activation(
+                    out=bias_y[:, n * F : (n + 1) * F], in_=pb[:], func=ACT.Identity, bias=-LAM, scale=1.0
+                )
 
         def load_w(b):
             if not ok(b):
@@ -81,25 +102,6 @@ def tile_afno2d_pb_kernel(tc, o1k, o1n, w2, b2, out):
                     in_=x_d[i][:, b, :].rearrange("(c p) f -> p c f", p=P),
                 )
                 st["x", i, b] = x
-
-        pbt = ps_t.tile([P, 4 * P], F32, name="pt")
-        nc.tensor.transpose(out=pbt[:, 0:P], in_=btile[:].bitcast(F32), identity=ident[:])
-        bsb = consts.tile([P, 2 * NB], F32, name="bsb")
-        nc.vector.tensor_copy(out=bsb[:], in_=pbt[:, 0 : 2 * NB])
-        bias0 = consts.tile([P, 4 * NB], F32, name="bias0")
-        nc.vector.tensor_copy(out=bias0[:], in_=bsb[:].bitcast(BF16))
-        bias_y = consts.tile([P, NB * F], F32, name="bias_y")
-        for n in range(NB):
-            pb = ps_y.tile([P, F], F32, name="py")
-            nc.tensor.matmul(
-                out=pb[:], lhsT=ones[:], rhs=brow[:, n * F : (n + 1) * F], start=True, stop=True
-            )
-            if n % 2 == 0:
-                nc.scalar.activation(
-                    out=bias_y[:, n * F : (n + 1) * F], in_=pb[:], func=ACT.Identity, bias=-LAM, scale=1.0
-                )
-            else:
-                nc.vector.tensor_scalar_add(out=bias_y[:, n * F : (n + 1) * F], in0=pb[:], scalar1=-LAM)
 
         def add_sub(b, which):
             if not ok(b):
@@ -285,6 +287,8 @@ def tile_afno2d_pb_kernel(tc, o1k, o1n, w2, b2, out):
         for i in range(-4, NB + 1):
             load_x(i + 3)
             load_w(i + 4)
+            if i == -3:
+                load_bias()
             transposes(i + 2, 0)
             evac1(i, (0, 1))
             stage1(i, (2, 3))
@@ -312,3 +316,8 @@ def tile_afno2d_pb_kernel(tc, o1k, o1n, w2, b2, out):
                     regroup_w(i + 3, which, e, "v")
             evac_x(i + 2, 1)
             y_bias(i)
+            if i == -2:
+                bias_columns()
+                bias_rows(range(0, NB // 2))
+            if i == -1:
+                bias_rows(range(NB // 2, NB))

@@ -31,7 +31,6 @@ def tile_afno2d_pb_kernel(tc, o1k, o1n, w2, b2, out):
     out_d = out.rearrange("b h w (n o) -> (b h w) n o", n=NB)
 
     with ExitStack() as ctx:
-        ctx.enter_context(tc.manual_schedule())
         consts = ctx.enter_context(tc.tile_pool(name="consts", bufs=1))
         loads = ctx.enter_context(tc.tile_pool(name="loads", bufs=3))
         work = ctx.enter_context(tc.tile_pool(name="work", bufs=2))
@@ -52,34 +51,13 @@ def tile_afno2d_pb_kernel(tc, o1k, o1n, w2, b2, out):
         nc.vector.memset(ones[:], 1.0)
         brow = consts.tile([P, NB * F], BF16, name="brow")
         nc.vector.memset(brow[:].bitcast(I32), 0)
+        nc.sync.dma_start(out=brow[0:2, :], in_=b2.rearrange("i n o -> i (n o)"))
         btile = consts.tile([P, 2 * P], BF16, name="btile")
         nc.vector.memset(btile[:].bitcast(I32), 0)
-        bsb = consts.tile([P, 2 * NB], F32, name="bsb")
-        bias0 = consts.tile([P, 4 * NB], F32, name="bias0")
-        bias_y = consts.tile([P, NB * F], F32, name="bias_y")
-
-        def load_bias():
-            nc.sync.dma_start(out=brow[0:2, :], in_=b2.rearrange("i n o -> i (n o)"))
-            nc.sync.dma_start(
-                out=btile[0 : 2 * NB, :],
-                in_=b2[0, :, :].rearrange("n (u r) -> (n u) r", u=2),
-            )
-
-        def bias_columns():
-            pbt = ps_s.tile([P, T], F32, name="ps1")
-            nc.tensor.transpose(out=pbt[:, 0:P], in_=btile[:].bitcast(F32), identity=ident[:])
-            nc.vector.tensor_copy(out=bsb[:], in_=pbt[:, 0 : 2 * NB])
-            nc.vector.tensor_copy(out=bias0[:], in_=bsb[:].bitcast(BF16))
-
-        def bias_rows(blocks):
-            for n in blocks:
-                pb = ps_y.tile([P, F], F32, name="py")
-                nc.tensor.matmul(
-                    out=pb[:], lhsT=ones[:], rhs=brow[:, n * F : (n + 1) * F], start=True, stop=True
-                )
-                nc.scalar.activation(
-                    out=bias_y[:, n * F : (n + 1) * F], in_=pb[:], func=ACT.Identity, bias=-LAM, scale=1.0
-                )
+        nc.sync.dma_start(
+            out=btile[0 : 2 * NB, :],
+            in_=b2[0, :, :].rearrange("n (u r) -> (n u) r", u=2),
+        )
 
         def load_w(b):
             if not ok(b):
@@ -102,6 +80,25 @@ def tile_afno2d_pb_kernel(tc, o1k, o1n, w2, b2, out):
                     in_=x_d[i][:, b, :].rearrange("(c p) f -> p c f", p=P),
                 )
                 st["x", i, b] = x
+
+        pbt = ps_t.tile([P, 4 * P], F32, name="pt")
+        nc.tensor.transpose(out=pbt[:, 0:P], in_=btile[:].bitcast(F32), identity=ident[:])
+        bsb = consts.tile([P, 2 * NB], F32, name="bsb")
+        nc.vector.tensor_copy(out=bsb[:], in_=pbt[:, 0 : 2 * NB])
+        bias0 = consts.tile([P, 4 * NB], F32, name="bias0")
+        nc.vector.tensor_copy(out=bias0[:], in_=bsb[:].bitcast(BF16))
+        bias_y = consts.tile([P, NB * F], F32, name="bias_y")
+        for n in range(NB):
+            pb = ps_y.tile([P, F], F32, name="py")
+            nc.tensor.matmul(
+                out=pb[:], lhsT=ones[:], rhs=brow[:, n * F : (n + 1) * F], start=True, stop=True
+            )
+            if n % 2 == 0:
+                nc.scalar.activation(
+                    out=bias_y[:, n * F : (n + 1) * F], in_=pb[:], func=ACT.Identity, bias=-LAM, scale=1.0
+                )
+            else:
+                nc.vector.tensor_scalar_add(out=bias_y[:, n * F : (n + 1) * F], in0=pb[:], scalar1=-LAM)
 
         def add_sub(b, which):
             if not ok(b):
@@ -287,8 +284,6 @@ def tile_afno2d_pb_kernel(tc, o1k, o1n, w2, b2, out):
         for i in range(-4, NB + 1):
             load_x(i + 3)
             load_w(i + 4)
-            if i == -3:
-                load_bias()
             transposes(i + 2, 0)
             evac1(i, (0, 1))
             stage1(i, (2, 3))
@@ -316,8 +311,3 @@ def tile_afno2d_pb_kernel(tc, o1k, o1n, w2, b2, out):
                     regroup_w(i + 3, which, e, "v")
             evac_x(i + 2, 1)
             y_bias(i)
-            if i == -2:
-                bias_columns()
-                bias_rows(range(0, NB // 2))
-            if i == -1:
-                bias_rows(range(NB // 2, NB))

@@ -17,6 +17,7 @@ NB = 8
 T = 512
 F = 512
 TC = T // P
+H = F // 2
 LAM = 0.01
 FLOPS = 4 * NB * 2 * T * F * F
 VECTOR_REGROUPS = (0,)
@@ -47,6 +48,10 @@ def tile_afno2d_pb_kernel(tc, o1k, o1n, w2, b2, out):
 
         ident = consts.tile([P, P], F32, name="ident")
         make_identity(nc, ident[:])
+        identb = consts.tile([P, P], BF16, name="identb")
+        make_identity(nc, identb[:])
+        negidb = consts.tile([P, P], BF16, name="negidb")
+        nc.vector.tensor_scalar_mul(out=negidb[:], in0=identb[:], scalar1=-1.0)
         ones = consts.tile([P, P], BF16, name="ones")
         nc.vector.memset(ones[:], 1.0)
         brow = consts.tile([P, NB * F], BF16, name="brow")
@@ -103,23 +108,53 @@ def tile_afno2d_pb_kernel(tc, o1k, o1n, w2, b2, out):
         def add_sub(b, which):
             if not ok(b):
                 return
-            r = work.tile([P, 4 * F], BF16, name="wr%d" % which)
-            nc.vector.tensor_tensor(
-                out=r[:],
-                in0=st["w", 0, b][:],
-                in1=st["w", 1, b][:],
-                op=(ALU.add if which == 0 else ALU.subtract),
-            )
+            if which == 0:
+                r = work.tile([P, 4 * F], BF16, name="wr0")
+                nc.vector.tensor_tensor(out=r[:], in0=st["w", 0, b][:], in1=st["w", 1, b][:], op=ALU.add)
+            else:
+                r = work.tile([P, 4 * H], BF16, name="wr1")
+                nc.vector.tensor_tensor(
+                    out=r[:].rearrange("p (t o) -> p t o", t=4),
+                    in0=st["w", 0, b][:].rearrange("p (t o) -> p t o", t=4)[:, :, 0:H],
+                    in1=st["w", 1, b][:].rearrange("p (t o) -> p t o", t=4)[:, :, 0:H],
+                    op=ALU.subtract,
+                )
             st["wr", which, b] = r
 
+        def sub_on_pe(b):
+            if not ok(b):
+                return
+            for e in range(2):
+                pw = ps_s.tile([P, T], F32, name="ps1")
+                for i in range(2):
+                    nc.tensor.matmul(
+                        out=pw[:].rearrange("p (t q) -> p t q", t=4),
+                        lhsT=(identb[:] if i == 0 else negidb[:]),
+                        rhs=st["w", i, b][:].rearrange("p (t q e) -> p e t q", t=4, e=2)[:, e, :, P : 2 * P],
+                        start=(i == 0),
+                        stop=(i == 1),
+                    )
+                st["pw", e, b] = pw
+
+        def evac_sub(b):
+            if not ok(b):
+                return
+            for e in range(2):
+                lo = 4 * F + e * 2 * F + F
+                nc.scalar.copy(
+                    out=st["wg", b][:, lo : lo + F].rearrange("p (q t) -> p q t", t=4),
+                    in_=st["pw", e, b][:].rearrange("p (t q) -> p q t", t=4),
+                )
+
         def regroup_w(b, which, e, engine):
-            on_vector = b in VECTOR_REGROUPS or (which == 1 and e == 1)
+            on_vector = b in VECTOR_REGROUPS or which == 1
             if not ok(b) or (engine == "v") != on_vector:
                 return
             if ("wg", b) not in st:
                 st["wg", b] = work.tile([P, 8 * F], BF16, name="wg", align_bytes=64)
-            g = st["wg", b][:, which * 4 * F : (which + 1) * 4 * F]
-            dst = g.rearrange("p (e c i t) -> p e c t i", e=2, i=4, t=4)[:, e]
+            width = 2 * F if which == 0 else F
+            lo = which * 4 * F + e * 2 * F
+            dst = st["wg", b][:, lo : lo + width].rearrange("p (c i t) -> p c t i", i=4, t=4)
             src = st["wr", which, b][:].rearrange("p (t c i e) -> p e c t i", t=4, i=4, e=2)[:, e]
             if engine == "v":
                 nc.vector.tensor_copy(out=dst, in_=src)
@@ -297,17 +332,17 @@ def tile_afno2d_pb_kernel(tc, o1k, o1n, w2, b2, out):
             evac_x(i + 2, 0)
             transposes(i + 2, 1)
             stage1(i + 1, (0, 1))
+            sub_on_pe(i + 2)
             add_sub(i + 3, 0)
             quantise_o2(i)
             y_neg(i - 1, 1)
             y_out(i - 1, 1)
             y_last(i)
             regroup_w(i + 2, 0, 1, "s")
-            regroup_w(i + 2, 1, 0, "s")
-            regroup_w(i + 2, 1, 1, "s")
             add_sub(i + 3, 1)
             for which in range(2):
                 for e in range(2):
                     regroup_w(i + 3, which, e, "v")
             evac_x(i + 2, 1)
+            evac_sub(i + 2)
             y_bias(i)

from contextlib import ExitStack

import concourse.mybir as mybir
from concourse.masks import make_identity

F32 = mybir.dt.float32
BF16 = mybir.dt.bfloat16
I32 = mybir.dt.int32
U32 = mybir.dt.uint32
U8 = mybir.dt.uint8
FP8X4 = mybir.dt.float8_e4m3fn_x4
ALU = mybir.AluOpType
ACT = mybir.ActivationFunctionType

P = 128
NB = 8
T = 512
F = 512
TC = T // P
H = F // 2
LAM = 0.01
FLOPS = 4 * NB * 2 * T * F * F
VECTOR_REGROUPS = (0,)


def tile_afno2d_pb_kernel(tc, o1k, o1n, w2, b2, out):
    nc = tc.nc
    x_d = (
        o1k.rearrange("b h w n f -> (b h w) n f"),
        o1n.rearrange("b h w n f -> (b h w) n f"),
    )
    out_d = out.rearrange("b h w (n o) -> (b h w) n o", n=NB)

    with ExitStack() as ctx:
        consts = ctx.enter_context(tc.tile_pool(name="consts", bufs=1))
        loads = ctx.enter_context(tc.tile_pool(name="loads", bufs=3))
        work = ctx.enter_context(tc.tile_pool(name="work", bufs=2))
        codes = ctx.enter_context(tc.tile_pool(name="codes", bufs=3))
        ypool = ctx.enter_context(tc.tile_pool(name="ypool", bufs=2))
        ps_t = ctx.enter_context(tc.psum_pool(name="ps_t", bufs=2))
        ps_s = ctx.enter_context(tc.psum_pool(name="ps_s", bufs=2))
        ps_y = ctx.enter_context(tc.psum_pool(name="ps_y", bufs=4))

        st = {}

        def ok(b):
            return 0 <= b < NB

        ident = consts.tile([P, P], F32, name="ident")
        make_identity(nc, ident[:])
        identb = consts.tile([P, P], BF16, name="identb")
        make_identity(nc, identb[:])
        negidb = consts.tile([P, P], BF16, name="negidb")
        nc.vector.tensor_scalar_mul(out=negidb[:], in0=identb[:], scalar1=-1.0)
        ones = consts.tile([P, P], BF16, name="ones")
        nc.vector.memset(ones[:], 1.0)
        brow = consts.tile([P, NB * F], BF16, name="brow")
        nc.vector.memset(brow[:].bitcast(I32), 0)
        nc.sync.dma_start(out=brow[0:2, :], in_=b2.rearrange("i n o -> i (n o)"))
        btile = consts.tile([P, 2 * P], BF16, name="btile")
        nc.vector.memset(btile[:].bitcast(I32), 0)
        nc.sync.dma_start(
            out=btile[0 : 2 * NB, :],
            in_=b2[0, :, :].rearrange("n (u r) -> (n u) r", u=2),
        )

        def load_w(b):
            if not ok(b):
                return
            for i in range(2):
                w = loads.tile([P, 4 * F], BF16, name="w%d" % i)
                nc.sync.dma_start(
                    out=w[:].rearrange("p (u r) -> p u r", u=2),
                    in_=w2[i, b, :, :].rearrange("(u p e) o -> p u (e o)", u=2, e=2),
                )
                st["w", i, b] = w

        def load_x(b):
            if not ok(b):
                return
            for i in range(2):
                x = loads.tile([P, TC * F], BF16, name="x%d" % i)
                nc.sync.dma_start(
                    out=x[:].rearrange("p (c f) -> p c f", c=TC),
                    in_=x_d[i][:, b, :].rearrange("(c p) f -> p c f", p=P),
                )
                st["x", i, b] = x

        pbt = ps_t.tile([P, 4 * P], F32, name="pt")
        nc.tensor.transpose(out=pbt[:, 0:P], in_=btile[:].bitcast(F32), identity=ident[:])
        bsb = consts.tile([P, 2 * NB], F32, name="bsb")
        nc.vector.tensor_copy(out=bsb[:], in_=pbt[:, 0 : 2 * NB])
        bias0 = consts.tile([P, 4 * NB], F32, name="bias0")
        nc.vector.tensor_copy(out=bias0[:], in_=bsb[:].bitcast(BF16))
        bias_y = consts.tile([P, NB * F], F32, name="bias_y")
        for n in range(NB):
            pb = ps_y.tile([P, F], F32, name="py")
            nc.tensor.matmul(
                out=pb[:], lhsT=ones[:], rhs=brow[:, n * F : (n + 1) * F], start=True, stop=True
            )
            if n % 2 == 0:
                nc.scalar.activation(
                    out=bias_y[:, n * F : (n + 1) * F], in_=pb[:], func=ACT.Identity, bias=-LAM, scale=1.0
                )
            else:
                nc.vector.tensor_scalar_add(out=bias_y[:, n * F : (n + 1) * F], in0=pb[:], scalar1=-LAM)

        def add_sub(b, which):
            if not ok(b):
                return
            if which == 0:
                r = work.tile([P, 4 * F], BF16, name="wr0")
                nc.vector.tensor_tensor(out=r[:], in0=st["w", 0, b][:], in1=st["w", 1, b][:], op=ALU.add)
            else:
                r = work.tile([P, 4 * H], BF16, name="wr1")
                nc.vector.tensor_tensor(
                    out=r[:].rearrange("p (t o) -> p t o", t=4),
                    in0=st["w", 0, b][:].rearrange("p (t o) -> p t o", t=4)[:, :, 0:H],
                    in1=st["w", 1, b][:].rearrange("p (t o) -> p t o", t=4)[:, :, 0:H],
                    op=ALU.subtract,
                )
            st["wr", which, b] = r

        def sub_on_pe(b):
            if not ok(b):
                return
            for e in range(2):
                pw = ps_s.tile([P, T], F32, name="ps1")
                for i in range(2):
                    nc.tensor.matmul(
                        out=pw[:].rearrange("p (t q) -> p t q", t=4),
                        lhsT=(identb[:] if i == 0 else negidb[:]),
                        rhs=st["w", i, b][:].rearrange("p (t q e) -> p e t q", t=4, e=2)[:, e, :, P : 2 * P],
                        start=(i == 0),
                        stop=(i == 1),
                    )
                st["pw", e, b] = pw

        def evac_sub(b):
            if not ok(b):
                return
            for e in range(2):
                lo = 4 * F + e * 2 * F + F
                nc.scalar.copy(
                    out=st["wg", b][:, lo : lo + F].rearrange("p (q t) -> p q t", t=4),
                    in_=st["pw", e, b][:].rearrange("p (t q) -> p q t", t=4),
                )

        def regroup_w(b, which, e, engine):
            on_vector = b in VECTOR_REGROUPS or which == 1
            if not ok(b) or (engine == "v") != on_vector:
                return
            if ("wg", b) not in st:
                st["wg", b] = work.tile([P, 8 * F], BF16, name="wg", align_bytes=64)
            width = 2 * F if which == 0 else F
            lo = which * 4 * F + e * 2 * F
            dst = st["wg", b][:, lo : lo + width].rearrange("p (c i t) -> p c t i", i=4, t=4)
            src = st["wr", which, b][:].rearrange("p (t c i e) -> p e c t i", t=4, i=4, e=2)[:, e]
            if engine == "v":
                nc.vector.tensor_copy(out=dst, in_=src)
            else:
                nc.scalar.copy(out=dst, in_=src)

        def transposes(b, i):
            if not ok(b):
                return
            xw = st["x", i, b][:].bitcast(F32)
            for h in range(2):
                pt = ps_t.tile([P, 4 * P], F32, name="pt")
                for cl in range(2):
                    for u in range(2):
                        c = 2 * h + cl
                        nc.tensor.transpose(
                            out=pt[:, (2 * cl + u) * P : (2 * cl + u + 1) * P],
                            in_=xw[:, c * 256 + u * P : c * 256 + (u + 1) * P],
                            identity=ident[:],
                        )
                st["pt", i, h, b] = pt

        def evac_x(b, i):
            if not ok(b):
                return
            if i == 0:
                st["xg", b] = work.tile([P, 8 * T], BF16, name="xg", align_bytes=64)
            gw = st["xg", b][:].bitcast(F32)
            for h in range(2):
                lo = i * 1024 + h * 512
                nc.scalar.copy(
                    out=gw[:, lo : lo + 512].rearrange("p (c t u) -> p c t u", c=2, u=2),
                    in_=st["pt", i, h, b][:].rearrange("p (c u t) -> p c t u", c=2, u=2),
                )

        def quantise(src, tag, width):
            c = codes.tile([P, width], U32, name=tag + "c", align_bytes=64)
            s = codes.tile([P, width], U8, name=tag + "s", align_bytes=64)
            nc.vector.quantize_mx(out=c[:].bitcast(FP8X4), scales=s[:], in_=src[:])
            return (c, s)

        def quantise_xw(b):
            if not ok(b):
                return
            st["qx", b] = quantise(st["xg", b], "x", 2 * T)
            st["qw", b] = quantise(st["wg", b], "w", 2 * F)

        def mx(acc, a, a_lo, b_, b_lo, start, stop):
            nc.tensor.matmul_mx(
                out=acc[:],
                lhsT=a[0][:, a_lo : a_lo + P].bitcast(FP8X4),
                lhsT_scale=a[1][:, a_lo : a_lo + P],
                rhs=b_[0][:, b_lo : b_lo + 512].bitcast(FP8X4),
                rhs_scale=b_[1][:, b_lo : b_lo + 512],
                start=start,
                stop=stop,
            )

        def stage1(b, chunks):
            if not ok(b):
                return
            qx, qw = st["qx", b], st["qw", b]
            for c in chunks:
                ps1 = ps_s.tile([P, T], F32, name="ps1")
                mx(ps1, qw, c * P, qx, 0, True, False)
                mx(ps1, qw, F + c * P, qx, T, False, True)
                st["ps1", c, b] = ps1

        def evac1(b, chunks):
            if not ok(b):
                return
            if chunks[0] == 0:
                st["o2b", b] = work.tile([P, 4 * T], BF16, name="o2b")
            for c in chunks:
                t4 = 2 * (c % 2) + c // 2
                nc.scalar.activation(
                    out=st["o2b", b][:, t4 * T : (t4 + 1) * T],
                    in_=st["ps1", c, b][:],
                    func=ACT.Identity,
                    bias=bias0[:, b * 4 + t4 : b * 4 + t4 + 1],
                    scale=0.5,
                )

        def regroup_o2(b):
            if not ok(b):
                return
            o2g = work.tile([P, 4 * T], BF16, name="o2g", align_bytes=64)
            nc.vector.tensor_copy(
                out=o2g[:].rearrange("p (c i j) -> p c j i", i=4, j=4),
                in_=st["o2b", b][:].rearrange("p (j c i) -> p c j i", i=4, j=4),
            )
            st["o2g", b] = o2g

        def quantise_o2(b):
            if not ok(b):
                return
            st["qo", b] = quantise(st["o2g", b], "o", T)

        def y_first(b):
            if not ok(b):
                return
            qx, qw = st["qx", b], st["qw", b]
            for c in range(TC):
                py = ps_y.tile([P, F], F32, name="py")
                mx(py, qx, c * P, qw, 0, True, False)
                mx(py, qx, T + c * P, qw, F, False, False)
                mx(py, qx, T + c * P, qw, 0, False, False)
                st["py", c, b] = py

        def y_last(b):
            if not ok(b):
                return
            for c in range(TC):
                mx(st["py", c, b], st["qo", b], c * P, st["qw", b], F, False, True)

        def y_bias(b):
            if not ok(b):
                return
            za = ypool.tile([P, TC * F], F32, name="za")
            for c in range(TC):
                nc.vector.scalar_tensor_tensor(
                    out=za[:, c * F : (c + 1) * F].rearrange("p (q e) -> p q e", e=2),
                    in0=st["py", c, b][:].rearrange("p (e q) -> p q e", e=2),
                    scalar=0.5,
                    in1=bias_y[:, b * F : (b + 1) * F].rearrange("p (q e) -> p q e", e=2),
                    op0=ALU.mult,
                    op1=ALU.add,
                )
            st["za", b] = za

        def y_pieces(b, h):
            n = 2 if b == NB - 1 else 1
            w = 2 // n
            return [
                (slice((2 * h + k * w) * F, (2 * h + (k + 1) * w) * F), slice((2 * h + k * w) * P, (2 * h + (k + 1) * w) * P))
                for k in range(n)
            ]

        def y_neg(b, h):
            if not ok(b):
                return
            if h == 0:
                st["r2", b] = ypool.tile([P, TC * F], F32, name="r2")
            for sl, rows in y_pieces(b, h):
                nc.scalar.activation(
                    out=st["r2", b][:, sl], in_=st["za", b][:, sl], func=ACT.Relu, bias=-2.0 * LAM, scale=-1.0
                )

        def y_out(b, h):
            if not ok(b):
                return
            r2 = st["r2", b]
            for sl, rows in y_pieces(b, h):
                nc.vector.scalar_tensor_tensor(
                    out=r2[:, sl], in0=st["za", b][:, sl], scalar=0.0, in1=r2[:, sl], op0=ALU.max, op1=ALU.subtract
                )
                nc.sync.dma_start(
                    out=out_d[rows, b, :].rearrange("(c p) o -> p c o", p=P),
                    in_=r2[:, sl].rearrange("p (c o) -> p c o", o=F),
                )

        for i in range(-4, NB + 1):
            load_x(i + 3)
            load_w(i + 4)
            transposes(i + 2, 0)
            evac1(i, (0, 1))
            stage1(i, (2, 3))
            quantise_xw(i + 1)
            regroup_w(i + 2, 0, 0, "s")
            y_neg(i - 1, 0)
            y_out(i - 1, 0)
            evac1(i, (2, 3))
            y_first(i)
            regroup_o2(i)
            evac_x(i + 2, 0)
            transposes(i + 2, 1)
            stage1(i + 1, (0, 1))
            sub_on_pe(i + 2)
            add_sub(i + 3, 0)
            quantise_o2(i)
            y_neg(i - 1, 1)
            y_out(i - 1, 1)
            y_last(i)
            regroup_w(i + 2, 0, 1, "s")
            add_sub(i + 3, 1)
            for which in range(2):
                for e in range(2):
                    regroup_w(i + 3, which, e, "v")
            evac_x(i + 2, 1)
            evac_sub(i + 2)
            y_bias(i)
